import numpy as np
import ml_dtypes


def mxq(x, axis, fmt="e4m3"):
    dtype, down = {"e4m3": (ml_dtypes.float8_e4m3fn, 7), "e5m2": (ml_dtypes.float8_e5m2, 14)}[fmt]
    v = np.moveaxis(np.asarray(x, np.float32).astype(ml_dtypes.bfloat16).astype(np.float64), axis, -1)
    blocks = v.reshape(v.shape[:-1] + (-1, 32))
    amax = np.abs(blocks).max(-1, keepdims=True)
    byte = np.maximum(np.where(amax > 0, np.frexp(amax)[1] - 1 + 127, 0) - down, 1)
    scale = np.exp2(byte - 127.0)
    codes = (blocks / scale).astype(np.float32).astype(dtype).astype(np.float64)
    return np.moveaxis((codes * scale).reshape(v.shape), -1, axis)


WIDE = False


def mx_kscale(k):
    if not WIDE:
        return np.ones(k)
    levels = np.array([10, -10, 5, -5, 0])
    a = np.random.permutation(np.resize(levels, k // 512 * 4)).reshape(k // 512, 4)
    idx = np.arange(k)
    return np.exp2(a[idx // 512, idx % 128 // 32])


BF16 = ml_dtypes.bfloat16


def bf(x):
    return np.asarray(x, np.float32).astype(BF16)


def f64(x):
    return np.asarray(x).astype(np.float64)


E2M1 = np.array([0.0, 0.5, 1.0, 1.5, 2.0, 3.0, 4.0, 6.0, -0.0, -0.5, -1.0, -1.5, -2.0, -3.0, -4.0, -6.0])


def pack_weight(w, fmt):
    k, n = w.shape
    w = f64(bf(w)).reshape(k // 32, 32, n)
    amax = np.abs(w).max(1)
    if fmt == "e4m3":
        byte = np.frexp(amax)[1] - 1 + 127 - 7
    else:
        mant, ex = np.frexp(amax / 6.0)
        byte = np.where(mant > 0.5, ex, ex - 1) + 127
    byte = np.clip(np.where(amax > 0, byte, 1), 1, 254)
    scaled = (w * np.exp2(127.0 - byte)[:, None, :]).reshape(k, n).astype(np.float32)
    by_word = np.ascontiguousarray(scaled.reshape(k // 512, 128, 4, n).transpose(0, 1, 3, 2))
    if fmt == "e4m3":
        words = by_word.astype(ml_dtypes.float8_e4m3fn).view(np.uint8)
    else:
        c = by_word.astype(ml_dtypes.float4_e2m1fn).view(np.uint8) & 0xF
        words = c[..., 0::2] | (c[..., 1::2] << 4)
    return np.ascontiguousarray(words), np.ascontiguousarray(byte.astype(np.uint8).reshape(k // 512, 16, n))


def unpack_weight(words, scales, fmt):
    g, p, n, _ = words.shape
    if fmt == "e4m3":
        vals = np.ascontiguousarray(words).view(ml_dtypes.float8_e4m3fn).astype(np.float64)
    else:
        nib = np.empty((g, p, n, 4), np.uint8)
        nib[..., 0::2] = words & 0xF
        nib[..., 1::2] = words >> 4
        vals = E2M1[nib]
    vals = vals * np.repeat(np.exp2(scales.astype(np.float64) - 127.0), 8, axis=1)[..., None]
    return vals.transpose(0, 1, 3, 2).reshape(g * 512, n)

def pack4(w):
    words, scales = pack_weight(w, "e2m1")
    return words.reshape(words.shape[0], 128, -1), scales


def unpack4(words, scales):
    return unpack_weight(words.reshape(words.shape[0], 128, -1, 2), scales, "e2m1")


B, T, D, H = 1, 512, 2048, 16
HD = D // H
SCALE = HD ** (-0.5)


def rotate_half(u):
    u1, u2 = np.split(u, 2, axis=-1)
    return np.concatenate([-u2, u1], axis=-1)


def apply_rope(u, sin, cos):
    return u * cos[None, :, None, :] + rotate_half(u) * sin[None, :, None, :]


def setup_inputs():
    s = mx_kscale(D)
    x = bf(np.random.standard_normal((B, T, D)) * s)
    sin = bf(np.random.standard_normal((T, HD)))
    cos = bf(np.random.standard_normal((T, HD)))
    words, scales = pack4(np.random.standard_normal((D, D + 2 * HD)) * 2.0 / np.sqrt(D) / s[:, None])
    return {"x": x,
            "sin": sin,
            "cos": cos,
            "W_qkv_words": words,
            "W_qkv_scales": scales}


def reference(x, sin, cos, W_qkv_words, W_qkv_scales):
    sin, cos = f64(sin), f64(cos)
    qkv = mxq(f64(x), 2, "e4m3") @ unpack4(W_qkv_words, W_qkv_scales)
    q, k, v = np.split(qkv, [D, D + HD], axis=-1)
    q = q.reshape(B, T, H, HD) * SCALE
    q_rot = np.ascontiguousarray(apply_rope(q, sin, cos).transpose(0, 2, 1, 3))
    k_rot = apply_rope(k[:, :, None, :], sin, cos)[:, :, 0, :]
    return q_rot, k_rot, v

@@ -1,0 +1,217 @@
+from contextlib import ExitStack
+
+import concourse.mybir as mybir
+from concourse.masks import make_identity
+
+F32 = mybir.dt.float32
+BF16 = mybir.dt.bfloat16
+I32 = mybir.dt.int32
+U32 = mybir.dt.uint32
+U8 = mybir.dt.uint8
+FP8X4 = mybir.dt.float8_e4m3fn_x4
+FP4X4 = mybir.dt.float4_e2m1fn_x4
+MULT = mybir.AluOpType.mult
+ADD = mybir.AluOpType.add
+
+P = 128
+T = 512
+D = 2048
+HD = 128
+HALF = HD // 2
+Q_HEADS = 16
+PACK = 4
+K_PASS = P * PACK
+PASSES = D // K_PASS
+WORDS_PASS = K_PASS // 2
+CHUNK_HEADS = 4
+CHUNK = CHUNK_HEADS * HD
+Q_CHUNKS = Q_HEADS // CHUNK_HEADS
+TILES = 2
+ROUNDS = T // (P * TILES)
+SCALE_ROWS = 4
+Q_SCALE = HD ** -0.5
+
+FLOPS = 2 * T * D * (Q_HEADS + 2) * HD
+
+
+def tile_multiqueryattention_pa_kernel(
+    tc, x, sin, cos, W_qkv_words, W_qkv_scales, out_0, out_1, out_2
+):
+    nc = tc.nc
+
+    x_tiles = x.rearrange("b (a p r) k -> (b a) r p k", p=P, r=TILES)
+    sin_rows = sin.rearrange("(a p r) d -> p a (r d)", p=P, r=TILES)
+    cos_rows = cos.rearrange("(a p r) d -> p a (r d)", p=P, r=TILES)
+    w_words_dram = W_qkv_words.bitcast(I32).rearrange("g p n -> p g n")
+    w_scales_dram = W_qkv_scales.bitcast(I32).rearrange("g (q j) n -> j q g n", j=SCALE_ROWS)
+    q_dram = out_0.rearrange(
+        "b (c h) (a p r) d -> (b c) a p h (r d)", h=CHUNK_HEADS, p=P, r=TILES
+    )
+    k_dram = out_1.rearrange("b (a p r) d -> (b a) p (r d)", p=P, r=TILES)
+    v_dram = out_2.rearrange("b (a p r) d -> (b a) p (r d)", p=P, r=TILES)
+
+    with ExitStack() as ctx:
+        keep = ctx.enter_context(tc.tile_pool(name="keep", bufs=1))
+        stage = ctx.enter_context(tc.tile_pool(name="stage", bufs=2))
+        products = ctx.enter_context(tc.tile_pool(name="products", bufs=4))
+        psum_turn = ctx.enter_context(tc.psum_pool(name="psum_turn", bufs=2))
+        psum_acc = ctx.enter_context(tc.psum_pool(name="psum_acc", bufs=6))
+
+        def load_tokens(a, r):
+            tokens = keep.tile([P, D], BF16, name="x_%d_%d" % (a, r))
+            nc.sync.dma_start(out=tokens[:], in_=x_tiles[a, r])
+            return tokens
+
+        def load_weight_columns(name, first, width):
+            planes = keep.tile([P, PASSES, width], U8, name="planes_" + name, align_bytes=64)
+            nc.vector.memset(planes[:].bitcast(I32), 0)
+            for j in range(SCALE_ROWS):
+                nc.sync.dma_start(
+                    out=planes[:].bitcast(I32)[j:P:32, :, :],
+                    in_=w_scales_dram[j, :, :, first // 4 : (first + width) // 4],
+                )
+            words = keep.tile([P, PASSES, 2 * width], U8, name="words_" + name, align_bytes=64)
+            nc.sync.dma_start(
+                out=words[:].bitcast(I32),
+                in_=w_words_dram[:, :, first // 2 : (first + width) // 2],
+            )
+            return words, planes
+
+        x_sb = [[None] * TILES for a in range(ROUNDS)]
+        weights = [None] * Q_CHUNKS
+        sin_sb = keep.tile([P, ROUNDS, TILES * HD], BF16, name="sin_sb")
+        cos_sb = keep.tile([P, ROUNDS, TILES * HD], BF16, name="cos_sb")
+        for r in range(TILES):
+            x_sb[0][r] = load_tokens(0, r)
+        nc.sync.dma_start(out=sin_sb[:], in_=sin_rows)
+        nc.sync.dma_start(out=cos_sb[:], in_=cos_rows)
+        for c in range(Q_CHUNKS - 1):
+            weights[c] = load_weight_columns("q%d" % c, c * CHUNK, CHUNK)
+        for a in range(1, ROUNDS):
+            for r in range(TILES):
+                x_sb[a][r] = load_tokens(a, r)
+        weights[Q_CHUNKS - 1] = load_weight_columns(
+            "q%d" % (Q_CHUNKS - 1), (Q_CHUNKS - 1) * CHUNK, CHUNK
+        )
+        kv_words, kv_planes = load_weight_columns("kv", Q_HEADS * HD, 2 * HD)
+
+        identity = keep.tile([P, P], F32, name="identity")
+        make_identity(nc, identity[:])
+
+        def build_table(name, factor):
+            table = keep.tile([P, ROUNDS, TILES, 2, HD], F32, name=name)
+            quarters = table[:].rearrange("p a r w (s i) -> p (a r) (w s) i", s=2)
+            cos_halves = cos_sb[:].rearrange("p a (r s i) -> p (a r) s i", s=2, i=HALF)
+            sin_halves = sin_sb[:].rearrange("p a (r s i) -> p (a r) s i", s=2, i=HALF)
+            nc.gpsimd.tensor_scalar(
+                out=quarters[:, :, 0:4:3, :], in0=cos_halves,
+                scalar1=factor, scalar2=0.0, op0=MULT, op1=ADD,
+            )
+            nc.gpsimd.tensor_scalar(
+                out=quarters[:, :, 1, :], in0=sin_halves[:, :, 0, :],
+                scalar1=-factor, scalar2=0.0, op0=MULT, op1=ADD,
+            )
+            nc.gpsimd.tensor_scalar(
+                out=quarters[:, :, 2, :], in0=sin_halves[:, :, 1, :],
+                scalar1=factor, scalar2=0.0, op0=MULT, op1=ADD,
+            )
+            return table
+
+        q_table = build_table("q_table", Q_SCALE)
+        k_table = build_table("k_table", 1.0)
+
+        x_codes = [[None] * TILES for a in range(ROUNDS)]
+        x_scales = [[None] * TILES for a in range(ROUNDS)]
+
+        def quantise_tokens(a, r):
+            x_words = x_sb[a][r][:].bitcast(F32)
+            grouped = stage.tile([P, PASSES, P, PACK], BF16, align_bytes=64)
+            grouped_words = grouped[:].bitcast(F32)
+            for first_pass in range(0, PASSES, 2):
+                turned = psum_turn.tile([P, 2, 2, P], F32)
+                for g in range(2):
+                    start_word = (first_pass + g) * WORDS_PASS
+                    for u in range(2):
+                        nc.tensor.transpose(
+                            turned[:, g, u, :],
+                            x_words[:, start_word + u : start_word + WORDS_PASS : 2],
+                            identity[:],
+                        )
+                nc.scalar.copy(
+                    out=grouped_words[:, first_pass : first_pass + 2, :, :],
+                    in_=turned[:].rearrange("p g u t -> p g t u"),
+                )
+            codes = keep.tile([P, PASSES * P], U32, name="x_codes_%d_%d" % (a, r), align_bytes=64)
+            scales = keep.tile([P, PASSES * P], U8, name="x_scales_%d_%d" % (a, r), align_bytes=64)
+            nc.vector.quantize_mx(
+                out=codes[:].bitcast(FP8X4),
+                scales=scales[:],
+                in_=grouped[:].rearrange("p g t e -> p (g t e)"),
+            )
+            x_codes[a][r] = codes
+            x_scales[a][r] = scales
+
+        def project(acc, a, r, words, planes, first, width):
+            for g in range(PASSES):
+                nc.tensor.matmul_mx(
+                    out=acc,
+                    lhsT=x_codes[a][r][:, g * P : (g + 1) * P].bitcast(FP8X4),
+                    lhsT_scale=x_scales[a][r][:, g * P : (g + 1) * P],
+                    rhs=words[:, g, 2 * first : 2 * (first + width)].bitcast(FP4X4),
+                    rhs_scale=planes[:, g, first : first + width],
+                    start=(g == 0),
+                    stop=(g == PASSES - 1),
+                )
+
+        def rotate(vectors, table, rotated):
+            n = vectors.shape[1]
+            prod = products.tile([P, CHUNK_HEADS, 2, HD], F32)
+            nc.vector.tensor_tensor(
+                out=prod[:, 0:n, :, :],
+                in0=vectors.unsqueeze(2).to_broadcast([P, n, 2, HD]),
+                in1=table,
+                op=MULT,
+            )
+            halves = prod[:, 0:n, :, :].rearrange("p n w (s i) -> p n w s i", s=2)
+            nc.gpsimd.tensor_tensor(
+                out=rotated.rearrange("p n (w i) -> p n w i", w=2),
+                in0=halves[:, :, :, 0, :],
+                in1=halves[:, :, :, 1, :],
+                op=ADD,
+            )
+
+        for r in range(TILES):
+            quantise_tokens(0, r)
+
+        for a in range(ROUNDS):
+            for c in range(Q_CHUNKS):
+                if c == Q_CHUNKS - 1 and a + 1 < ROUNDS:
+                    for r in range(TILES):
+                        quantise_tokens(a + 1, r)
+                words, planes = weights[c]
+                q_out = keep.tile([P, CHUNK_HEADS, TILES, HD], F32, name="q_out_%d_%d" % (a, c))
+                for r in range(TILES):
+                    acc = psum_acc.tile([P, CHUNK], F32)
+                    project(acc[:], a, r, words, planes, 0, CHUNK)
+                    rotate(
+                        acc[:].rearrange("p (h d) -> p h d", d=HD),
+                        q_table[:, a, r, :, :].unsqueeze(1).to_broadcast([P, CHUNK_HEADS, 2, HD]),
+                        q_out[:, :, r, :],
+                    )
+                nc.sync.dma_start(out=q_dram[c, a], in_=q_out[:].rearrange("p h r d -> p h (r d)"))
+
+            k_acc = psum_acc.tile([P, CHUNK], F32, tag="acc")
+            v_acc = psum_acc.tile([P, CHUNK], F32, tag="acc")
+            for r in range(TILES):
+                project(k_acc[:, r * HD : (r + 1) * HD], a, r, kv_words, kv_planes, 0, HD)
+                project(v_acc[:, r * HD : (r + 1) * HD], a, r, kv_words, kv_planes, HD, HD)
+            k_out = keep.tile([P, TILES, HD], F32, name="k_out_%d" % a)
+            rotate(
+                k_acc[:, 0 : TILES * HD].rearrange("p (r d) -> p r d", d=HD),
+                k_table[:, a, :, :, :],
+                k_out[:],
+            )
+            nc.sync.dma_start(out=k_dram[a], in_=k_out[:].rearrange("p r d -> p (r d)"))
+            v_out = keep.tile([P, TILES * HD], F32, name="v_out_%d" % a)
+            nc.scalar.copy(out=v_out[:], in_=v_acc[:, 0 : TILES * HD])
+            nc.sync.dma_start(out=v_dram[a], in_=v_out[:])

@@ -47,13 +47,13 @@ def tile_multiqueryattention_pa_kernel(
     q_dram = out_0.rearrange(
         "b (c h) (a p r) d -> (b c) a p h (r d)", h=CHUNK_HEADS, p=P, r=TILES
     )
-    k_dram = out_1.rearrange("b (a p r) d -> (b a) p (r d)", p=P, r=TILES)
-    v_dram = out_2.rearrange("b (a p r) d -> (b a) p (r d)", p=P, r=TILES)
+    k_dram = out_1.rearrange("b (a p r) d -> p (b a) (r d)", p=P, r=TILES)
+    v_dram = out_2.rearrange("b (a p r) d -> p (b a) (r d)", p=P, r=TILES)
 
     with ExitStack() as ctx:
         keep = ctx.enter_context(tc.tile_pool(name="keep", bufs=1))
-        stage = ctx.enter_context(tc.tile_pool(name="stage", bufs=2))
-        products = ctx.enter_context(tc.tile_pool(name="products", bufs=4))
+        stage = ctx.enter_context(tc.tile_pool(name="stage", bufs=3))
+        products = ctx.enter_context(tc.tile_pool(name="products", bufs=3))
         psum_turn = ctx.enter_context(tc.psum_pool(name="psum_turn", bufs=2))
         psum_acc = ctx.enter_context(tc.psum_pool(name="psum_acc", bufs=6))
 
@@ -85,14 +85,12 @@ def tile_multiqueryattention_pa_kernel(
             x_sb[0][r] = load_tokens(0, r)
         nc.sync.dma_start(out=sin_sb[:], in_=sin_rows)
         nc.sync.dma_start(out=cos_sb[:], in_=cos_rows)
-        for c in range(Q_CHUNKS - 1):
-            weights[c] = load_weight_columns("q%d" % c, c * CHUNK, CHUNK)
+        weights[0] = load_weight_columns("q0", 0, CHUNK)
         for a in range(1, ROUNDS):
             for r in range(TILES):
                 x_sb[a][r] = load_tokens(a, r)
-        weights[Q_CHUNKS - 1] = load_weight_columns(
-            "q%d" % (Q_CHUNKS - 1), (Q_CHUNKS - 1) * CHUNK, CHUNK
-        )
+        for c in range(1, Q_CHUNKS):
+            weights[c] = load_weight_columns("q%d" % c, c * CHUNK, CHUNK)
         kv_words, kv_planes = load_weight_columns("kv", Q_HEADS * HD, 2 * HD)
 
         identity = keep.tile([P, P], F32, name="identity")
@@ -125,9 +123,10 @@ def tile_multiqueryattention_pa_kernel(
 
         def quantise_tokens(a, r):
             x_words = x_sb[a][r][:].bitcast(F32)
-            grouped = stage.tile([P, PASSES, P, PACK], BF16, align_bytes=64)
-            grouped_words = grouped[:].bitcast(F32)
+            codes = keep.tile([P, PASSES, P], U32, name="x_codes_%d_%d" % (a, r), align_bytes=64)
+            scales = keep.tile([P, PASSES, P], U8, name="x_scales_%d_%d" % (a, r), align_bytes=64)
             for first_pass in range(0, PASSES, 2):
+                two_passes = slice(first_pass, first_pass + 2)
                 turned = psum_turn.tile([P, 2, 2, P], F32)
                 for g in range(2):
                     start_word = (first_pass + g) * WORDS_PASS
@@ -137,17 +136,15 @@ def tile_multiqueryattention_pa_kernel(
                             x_words[:, start_word + u : start_word + WORDS_PASS : 2],
                             identity[:],
                         )
+                grouped = stage.tile([P, 2, P, PACK], BF16, align_bytes=64)
                 nc.scalar.copy(
-                    out=grouped_words[:, first_pass : first_pass + 2, :, :],
-                    in_=turned[:].rearrange("p g u t -> p g t u"),
+                    out=grouped[:].bitcast(F32), in_=turned[:].rearrange("p g u t -> p g t u")
                 )
-            codes = keep.tile([P, PASSES * P], U32, name="x_codes_%d_%d" % (a, r), align_bytes=64)
-            scales = keep.tile([P, PASSES * P], U8, name="x_scales_%d_%d" % (a, r), align_bytes=64)
-            nc.vector.quantize_mx(
-                out=codes[:].bitcast(FP8X4),
-                scales=scales[:],
-                in_=grouped[:].rearrange("p g t e -> p (g t e)"),
-            )
+                nc.vector.quantize_mx(
+                    out=codes[:, two_passes, :].rearrange("p g t -> p (g t)").bitcast(FP8X4),
+                    scales=scales[:, two_passes, :].rearrange("p g t -> p (g t)"),
+                    in_=grouped[:].rearrange("p g t e -> p (g t e)"),
+                )
             x_codes[a][r] = codes
             x_scales[a][r] = scales
 
@@ -155,28 +152,27 @@ def tile_multiqueryattention_pa_kernel(
             for g in range(PASSES):
                 nc.tensor.matmul_mx(
                     out=acc,
-                    lhsT=x_codes[a][r][:, g * P : (g + 1) * P].bitcast(FP8X4),
-                    lhsT_scale=x_scales[a][r][:, g * P : (g + 1) * P],
+                    lhsT=x_codes[a][r][:, g, :].bitcast(FP8X4),
+                    lhsT_scale=x_scales[a][r][:, g, :],
                     rhs=words[:, g, 2 * first : 2 * (first + width)].bitcast(FP4X4),
                     rhs_scale=planes[:, g, first : first + width],
                     start=(g == 0),
                     stop=(g == PASSES - 1),
                 )
 
-        def rotate(vectors, table, rotated):
-            n = vectors.shape[1]
-            prod = products.tile([P, CHUNK_HEADS, 2, HD], F32)
+        def multiply(vectors, table, prod):
             nc.vector.tensor_tensor(
-                out=prod[:, 0:n, :, :],
-                in0=vectors.unsqueeze(2).to_broadcast([P, n, 2, HD]),
+                out=prod,
+                in0=vectors.unsqueeze(2).to_broadcast(list(prod.shape)),
                 in1=table,
                 op=MULT,
             )
-            halves = prod[:, 0:n, :, :].rearrange("p n w (s i) -> p n w s i", s=2)
-            nc.gpsimd.tensor_tensor(
-                out=rotated.rearrange("p n (w i) -> p n w i", w=2),
-                in0=halves[:, :, :, 0, :],
-                in1=halves[:, :, :, 1, :],
+
+        def add_halves(engine, prod, rotated):
+            engine.tensor_tensor(
+                out=rotated,
+                in0=prod[:, :, :, :, 0:HALF],
+                in1=prod[:, :, :, :, HALF:HD],
                 op=ADD,
             )
 
@@ -185,33 +181,42 @@ def tile_multiqueryattention_pa_kernel(
 
         for a in range(ROUNDS):
             for c in range(Q_CHUNKS):
-                if c == Q_CHUNKS - 1 and a + 1 < ROUNDS:
-                    for r in range(TILES):
-                        quantise_tokens(a + 1, r)
                 words, planes = weights[c]
                 q_out = keep.tile([P, CHUNK_HEADS, TILES, HD], F32, name="q_out_%d_%d" % (a, c))
+                q_prod = products.tile([P, TILES, CHUNK_HEADS, 2, HD], F32)
                 for r in range(TILES):
                     acc = psum_acc.tile([P, CHUNK], F32)
                     project(acc[:], a, r, words, planes, 0, CHUNK)
-                    rotate(
+                    multiply(
                         acc[:].rearrange("p (h d) -> p h d", d=HD),
                         q_table[:, a, r, :, :].unsqueeze(1).to_broadcast([P, CHUNK_HEADS, 2, HD]),
-                        q_out[:, :, r, :],
+                        q_prod[:, r, :, :, :],
                     )
+                add_halves(
+                    nc.gpsimd, q_prod[:], q_out[:].rearrange("p h r (w i) -> p r h w i", w=2)
+                )
                 nc.sync.dma_start(out=q_dram[c, a], in_=q_out[:].rearrange("p h r d -> p h (r d)"))
+                if c == 0 and a + 1 < ROUNDS:
+                    for r in range(TILES):
+                        quantise_tokens(a + 1, r)
 
-            k_acc = psum_acc.tile([P, CHUNK], F32, tag="acc")
-            v_acc = psum_acc.tile([P, CHUNK], F32, tag="acc")
+        k_acc = psum_acc.tile([P, ROUNDS, TILES, HD], F32, tag="acc")
+        v_acc = psum_acc.tile([P, ROUNDS, TILES, HD], F32, tag="acc")
+        for a in range(ROUNDS):
             for r in range(TILES):
-                project(k_acc[:, r * HD : (r + 1) * HD], a, r, kv_words, kv_planes, 0, HD)
-                project(v_acc[:, r * HD : (r + 1) * HD], a, r, kv_words, kv_planes, HD, HD)
-            k_out = keep.tile([P, TILES, HD], F32, name="k_out_%d" % a)
-            rotate(
-                k_acc[:, 0 : TILES * HD].rearrange("p (r d) -> p r d", d=HD),
-                k_table[:, a, :, :, :],
-                k_out[:],
-            )
-            nc.sync.dma_start(out=k_dram[a], in_=k_out[:].rearrange("p r d -> p (r d)"))
-            v_out = keep.tile([P, TILES * HD], F32, name="v_out_%d" % a)
-            nc.scalar.copy(out=v_out[:], in_=v_acc[:, 0 : TILES * HD])
-            nc.sync.dma_start(out=v_dram[a], in_=v_out[:])
+                project(k_acc[:, a, r, :], a, r, kv_words, kv_planes, 0, HD)
+        for a in range(ROUNDS):
+            for r in range(TILES):
+                project(v_acc[:, a, r, :], a, r, kv_words, kv_planes, HD, HD)
+        k_prod = keep.tile([P, ROUNDS, TILES, 2, HD], F32, name="k_prod")
+        multiply(
+            k_acc[:].rearrange("p a r d -> p (a r) d"),
+            k_table[:].rearrange("p a r w d -> p (a r) w d"),
+            k_prod[:].rearrange("p a r w d -> p (a r) w d"),
+        )
+        k_out = keep.tile([P, ROUNDS, TILES, HD], F32, name="k_out")
+        add_halves(nc.vector, k_prod[:], k_out[:].rearrange("p a r (w i) -> p a r w i", w=2))
+        nc.sync.dma_start(out=k_dram, in_=k_out[:].rearrange("p a r d -> p a (r d)"))
+        v_out = keep.tile([P, ROUNDS, TILES * HD], F32, name="v_out")
+        nc.scalar.copy(out=v_out[:], in_=v_acc[:].rearrange("p a r d -> p a (r d)"))
+        nc.sync.dma_start(out=v_dram, in_=v_out[:])

@@ -22,13 +22,13 @@ Q_HEADS = 16
 PACK = 4
 K_PASS = P * PACK
 PASSES = D // K_PASS
-WORDS_PASS = K_PASS // 2
 CHUNK_HEADS = 4
 CHUNK = CHUNK_HEADS * HD
 Q_CHUNKS = Q_HEADS // CHUNK_HEADS
 TILES = 2
-ROUNDS = T // (P * TILES)
+GROUPS = T // (P * TILES)
 SCALE_ROWS = 4
+PSUM_BANKS = 8
 Q_SCALE = HD ** -0.5
 
 FLOPS = 2 * T * D * (Q_HEADS + 2) * HD
@@ -50,17 +50,14 @@ def tile_multiqueryattention_pa_kernel(
     k_dram = out_1.rearrange("b (a p r) d -> p (b a) (r d)", p=P, r=TILES)
     v_dram = out_2.rearrange("b (a p r) d -> p (b a) (r d)", p=P, r=TILES)
 
+    token_tiles = [(a, r) for a in range(GROUPS) for r in range(TILES)]
+
     with ExitStack() as ctx:
+        ctx.enter_context(tc.manual_schedule())
         keep = ctx.enter_context(tc.tile_pool(name="keep", bufs=1))
         stage = ctx.enter_context(tc.tile_pool(name="stage", bufs=3))
         products = ctx.enter_context(tc.tile_pool(name="products", bufs=3))
-        psum_turn = ctx.enter_context(tc.psum_pool(name="psum_turn", bufs=2))
-        psum_acc = ctx.enter_context(tc.psum_pool(name="psum_acc", bufs=6))
-
-        def load_tokens(a, r):
-            tokens = keep.tile([P, D], BF16, name="x_%d_%d" % (a, r))
-            nc.sync.dma_start(out=tokens[:], in_=x_tiles[a, r])
-            return tokens
+        banks = ctx.enter_context(tc.psum_pool(name="banks", bufs=PSUM_BANKS))
 
         def load_weight_columns(name, first, width):
             planes = keep.tile([P, PASSES, width], U8, name="planes_" + name, align_bytes=64)
@@ -77,27 +74,24 @@ def tile_multiqueryattention_pa_kernel(
             )
             return words, planes
 
-        x_sb = [[None] * TILES for a in range(ROUNDS)]
-        weights = [None] * Q_CHUNKS
-        sin_sb = keep.tile([P, ROUNDS, TILES * HD], BF16, name="sin_sb")
-        cos_sb = keep.tile([P, ROUNDS, TILES * HD], BF16, name="cos_sb")
-        for r in range(TILES):
-            x_sb[0][r] = load_tokens(0, r)
+        x_sb = {}
+        for a, r in token_tiles:
+            x_sb[a, r] = keep.tile([P, D], BF16, name="x_%d_%d" % (a, r))
+            nc.sync.dma_start(out=x_sb[a, r][:], in_=x_tiles[a, r])
+        sin_sb = keep.tile([P, GROUPS, TILES * HD], BF16, name="sin_sb")
+        cos_sb = keep.tile([P, GROUPS, TILES * HD], BF16, name="cos_sb")
         nc.sync.dma_start(out=sin_sb[:], in_=sin_rows)
         nc.sync.dma_start(out=cos_sb[:], in_=cos_rows)
-        weights[0] = load_weight_columns("q0", 0, CHUNK)
-        for a in range(1, ROUNDS):
-            for r in range(TILES):
-                x_sb[a][r] = load_tokens(a, r)
-        for c in range(1, Q_CHUNKS):
-            weights[c] = load_weight_columns("q%d" % c, c * CHUNK, CHUNK)
+        q_weights = [
+            load_weight_columns("q%d" % c, c * CHUNK, CHUNK) for c in range(Q_CHUNKS)
+        ]
         kv_words, kv_planes = load_weight_columns("kv", Q_HEADS * HD, 2 * HD)
 
         identity = keep.tile([P, P], F32, name="identity")
         make_identity(nc, identity[:])
 
         def build_table(name, factor):
-            table = keep.tile([P, ROUNDS, TILES, 2, HD], F32, name=name)
+            table = keep.tile([P, GROUPS, TILES, 2, HD], F32, name=name)
             quarters = table[:].rearrange("p a r w (s i) -> p (a r) (w s) i", s=2)
             cos_halves = cos_sb[:].rearrange("p a (r s i) -> p (a r) s i", s=2, i=HALF)
             sin_halves = sin_sb[:].rearrange("p a (r s i) -> p (a r) s i", s=2, i=HALF)
@@ -118,23 +112,27 @@ def tile_multiqueryattention_pa_kernel(
         q_table = build_table("q_table", Q_SCALE)
         k_table = build_table("k_table", 1.0)
 
-        x_codes = [[None] * TILES for a in range(ROUNDS)]
-        x_scales = [[None] * TILES for a in range(ROUNDS)]
+        x_sorted = {}
+        x_codes = {}
+        x_scales = {}
+
+        def sort_words(a, r):
+            x_sorted[a, r] = keep.tile([P, PASSES, 2, P], F32, name="x_sorted_%d_%d" % (a, r))
+            nc.vector.tensor_copy(
+                out=x_sorted[a, r][:],
+                in_=x_sb[a, r][:].bitcast(F32).rearrange("t (g p u) -> t g u p", p=P, u=2),
+            )
 
         def quantise_tokens(a, r):
-            x_words = x_sb[a][r][:].bitcast(F32)
             codes = keep.tile([P, PASSES, P], U32, name="x_codes_%d_%d" % (a, r), align_bytes=64)
             scales = keep.tile([P, PASSES, P], U8, name="x_scales_%d_%d" % (a, r), align_bytes=64)
             for first_pass in range(0, PASSES, 2):
                 two_passes = slice(first_pass, first_pass + 2)
-                turned = psum_turn.tile([P, 2, 2, P], F32)
+                turned = banks.tile([P, 2, 2, P], F32, tag="bank")
                 for g in range(2):
-                    start_word = (first_pass + g) * WORDS_PASS
                     for u in range(2):
                         nc.tensor.transpose(
-                            turned[:, g, u, :],
-                            x_words[:, start_word + u : start_word + WORDS_PASS : 2],
-                            identity[:],
+                            turned[:, g, u, :], x_sorted[a, r][:, first_pass + g, u, :], identity[:]
                         )
                 grouped = stage.tile([P, 2, P, PACK], BF16, align_bytes=64)
                 nc.scalar.copy(
@@ -145,15 +143,15 @@ def tile_multiqueryattention_pa_kernel(
                     scales=scales[:, two_passes, :].rearrange("p g t -> p (g t)"),
                     in_=grouped[:].rearrange("p g t e -> p (g t e)"),
                 )
-            x_codes[a][r] = codes
-            x_scales[a][r] = scales
+            x_codes[a, r] = codes
+            x_scales[a, r] = scales
 
         def project(acc, a, r, words, planes, first, width):
             for g in range(PASSES):
                 nc.tensor.matmul_mx(
                     out=acc,
-                    lhsT=x_codes[a][r][:, g, :].bitcast(FP8X4),
-                    lhsT_scale=x_scales[a][r][:, g, :],
+                    lhsT=x_codes[a, r][:, g, :].bitcast(FP8X4),
+                    lhsT_scale=x_scales[a, r][:, g, :],
                     rhs=words[:, g, 2 * first : 2 * (first + width)].bitcast(FP4X4),
                     rhs_scale=planes[:, g, first : first + width],
                     start=(g == 0),
@@ -176,47 +174,48 @@ def tile_multiqueryattention_pa_kernel(
                 op=ADD,
             )
 
-        for r in range(TILES):
-            quantise_tokens(0, r)
+        sort_words(*token_tiles[0])
+        for n, (a, r) in enumerate(token_tiles):
+            if n + 1 < len(token_tiles):
+                sort_words(*token_tiles[n + 1])
+            quantise_tokens(a, r)
 
-        for a in range(ROUNDS):
-            for c in range(Q_CHUNKS):
-                words, planes = weights[c]
-                q_out = keep.tile([P, CHUNK_HEADS, TILES, HD], F32, name="q_out_%d_%d" % (a, c))
+        for c in range(Q_CHUNKS):
+            words, planes = q_weights[c]
+            for a in range(GROUPS):
                 q_prod = products.tile([P, TILES, CHUNK_HEADS, 2, HD], F32)
                 for r in range(TILES):
-                    acc = psum_acc.tile([P, CHUNK], F32)
+                    acc = banks.tile([P, CHUNK], F32, tag="bank")
                     project(acc[:], a, r, words, planes, 0, CHUNK)
                     multiply(
                         acc[:].rearrange("p (h d) -> p h d", d=HD),
                         q_table[:, a, r, :, :].unsqueeze(1).to_broadcast([P, CHUNK_HEADS, 2, HD]),
                         q_prod[:, r, :, :, :],
                     )
+                last_group = c == Q_CHUNKS - 1 and a == GROUPS - 1
+                q_out = keep.tile([P, CHUNK_HEADS, TILES, HD], F32, name="q_out_%d_%d" % (c, a))
                 add_halves(
-                    nc.gpsimd, q_prod[:], q_out[:].rearrange("p h r (w i) -> p r h w i", w=2)
+                    nc.vector if last_group else nc.gpsimd,
+                    q_prod[:],
+                    q_out[:].rearrange("p h r (w i) -> p r h w i", w=2),
                 )
                 nc.sync.dma_start(out=q_dram[c, a], in_=q_out[:].rearrange("p h r d -> p h (r d)"))
-                if c == 0 and a + 1 < ROUNDS:
-                    for r in range(TILES):
-                        quantise_tokens(a + 1, r)
 
-        k_acc = psum_acc.tile([P, ROUNDS, TILES, HD], F32, tag="acc")
-        v_acc = psum_acc.tile([P, ROUNDS, TILES, HD], F32, tag="acc")
-        for a in range(ROUNDS):
-            for r in range(TILES):
-                project(k_acc[:, a, r, :], a, r, kv_words, kv_planes, 0, HD)
-        for a in range(ROUNDS):
-            for r in range(TILES):
-                project(v_acc[:, a, r, :], a, r, kv_words, kv_planes, HD, HD)
-        k_prod = keep.tile([P, ROUNDS, TILES, 2, HD], F32, name="k_prod")
+        k_acc = banks.tile([P, GROUPS, TILES, HD], F32, tag="bank")
+        v_acc = banks.tile([P, GROUPS, TILES, HD], F32, tag="bank")
+        for a, r in token_tiles:
+            project(k_acc[:, a, r, :], a, r, kv_words, kv_planes, 0, HD)
+        for a, r in token_tiles:
+            project(v_acc[:, a, r, :], a, r, kv_words, kv_planes, HD, HD)
+        k_prod = keep.tile([P, GROUPS, TILES, 2, HD], F32, name="k_prod")
         multiply(
             k_acc[:].rearrange("p a r d -> p (a r) d"),
             k_table[:].rearrange("p a r w d -> p (a r) w d"),
             k_prod[:].rearrange("p a r w d -> p (a r) w d"),
         )
-        k_out = keep.tile([P, ROUNDS, TILES, HD], F32, name="k_out")
+        k_out = keep.tile([P, GROUPS, TILES, HD], F32, name="k_out")
         add_halves(nc.vector, k_prod[:], k_out[:].rearrange("p a r (w i) -> p a r w i", w=2))
         nc.sync.dma_start(out=k_dram, in_=k_out[:].rearrange("p a r d -> p a (r d)"))
-        v_out = keep.tile([P, ROUNDS, TILES * HD], F32, name="v_out")
+        v_out = keep.tile([P, GROUPS, TILES * HD], F32, name="v_out")
         nc.scalar.copy(out=v_out[:], in_=v_acc[:].rearrange("p a r d -> p a (r d)"))
         nc.sync.dma_start(out=v_dram, in_=v_out[:])

@@ -59,6 +59,9 @@ def tile_multiqueryattention_pa_kernel(
         products = ctx.enter_context(tc.tile_pool(name="products", bufs=3))
         banks = ctx.enter_context(tc.psum_pool(name="banks", bufs=PSUM_BANKS))
 
+        warm = keep.tile([P, CHUNK], BF16, name="warm")
+        nc.vector.memset(warm[:], 0.0)
+
         def load_weight_columns(name, first, width):
             planes = keep.tile([P, PASSES, width], U8, name="planes_" + name, align_bytes=64)
             nc.vector.memset(planes[:].bitcast(I32), 0)
@@ -111,6 +114,13 @@ def tile_multiqueryattention_pa_kernel(
 
         q_table = build_table("q_table", Q_SCALE)
         k_table = build_table("k_table", 1.0)
+
+        def warm_up(count):
+            unread = banks.tile([P, CHUNK], F32, tag="bank")
+            for n in range(count):
+                nc.tensor.matmul(
+                    out=unread[:], lhsT=warm[:, 0:P], rhs=warm[:], start=True, stop=True
+                )
 
         x_sorted = {}
         x_codes = {}
@@ -174,11 +184,13 @@ def tile_multiqueryattention_pa_kernel(
                 op=ADD,
             )
 
+        warm_up(6)
         sort_words(*token_tiles[0])
         for n, (a, r) in enumerate(token_tiles):
             if n + 1 < len(token_tiles):
                 sort_words(*token_tiles[n + 1])
             quantise_tokens(a, r)
+            warm_up(1 if n + 1 < len(token_tiles) else 3)
 
         for c in range(Q_CHUNKS):
             words, planes = q_weights[c]

@@ -81,6 +81,7 @@ def tile_multiqueryattention_pa_kernel(
         for a, r in token_tiles:
             x_sb[a, r] = keep.tile([P, D], BF16, name="x_%d_%d" % (a, r))
             nc.sync.dma_start(out=x_sb[a, r][:], in_=x_tiles[a, r])
+        kv_words, kv_planes = load_weight_columns("kv", Q_HEADS * HD, 2 * HD)
         sin_sb = keep.tile([P, GROUPS, TILES * HD], BF16, name="sin_sb")
         cos_sb = keep.tile([P, GROUPS, TILES * HD], BF16, name="cos_sb")
         nc.sync.dma_start(out=sin_sb[:], in_=sin_rows)
@@ -88,7 +89,6 @@ def tile_multiqueryattention_pa_kernel(
         q_weights = [
             load_weight_columns("q%d" % c, c * CHUNK, CHUNK) for c in range(Q_CHUNKS)
         ]
-        kv_words, kv_planes = load_weight_columns("kv", Q_HEADS * HD, 2 * HD)
 
         identity = keep.tile([P, P], F32, name="identity")
         make_identity(nc, identity[:])
@@ -112,8 +112,8 @@ def tile_multiqueryattention_pa_kernel(
             )
             return table
 
-        q_table = build_table("q_table", Q_SCALE)
         k_table = build_table("k_table", 1.0)
+        q_table = build_table("q_table", Q_SCALE)
 
         def warm_up(count):
             unread = banks.tile([P, CHUNK], F32, tag="bank")
@@ -190,8 +190,23 @@ def tile_multiqueryattention_pa_kernel(
             if n + 1 < len(token_tiles):
                 sort_words(*token_tiles[n + 1])
             quantise_tokens(a, r)
-            warm_up(1 if n + 1 < len(token_tiles) else 3)
+            if n + 1 < len(token_tiles):
+                warm_up(1)
 
+        k_acc = banks.tile([P, GROUPS, TILES, HD], F32, tag="bank")
+        for a, r in token_tiles:
+            project(k_acc[:, a, r, :], a, r, kv_words, kv_planes, 0, HD)
+        k_prod = keep.tile([P, GROUPS, TILES, 2, HD], F32, name="k_prod")
+        multiply(
+            k_acc[:].rearrange("p a r d -> p (a r) d"),
+            k_table[:].rearrange("p a r w d -> p (a r) w d"),
+            k_prod[:].rearrange("p a r w d -> p (a r) w d"),
+        )
+        k_out = keep.tile([P, GROUPS, TILES, HD], F32, name="k_out")
+        add_halves(nc.gpsimd, k_prod[:], k_out[:].rearrange("p a r (w i) -> p a r w i", w=2))
+        nc.sync.dma_start(out=k_dram, in_=k_out[:].rearrange("p a r d -> p a (r d)"))
+
+        left_to_vector = []
         for c in range(Q_CHUNKS):
             words, planes = q_weights[c]
             for a in range(GROUPS):
@@ -204,30 +219,33 @@ def tile_multiqueryattention_pa_kernel(
                         q_table[:, a, r, :, :].unsqueeze(1).to_broadcast([P, CHUNK_HEADS, 2, HD]),
                         q_prod[:, r, :, :, :],
                     )
-                last_group = c == Q_CHUNKS - 1 and a == GROUPS - 1
                 q_out = keep.tile([P, CHUNK_HEADS, TILES, HD], F32, name="q_out_%d_%d" % (c, a))
-                add_halves(
-                    nc.vector if last_group else nc.gpsimd,
-                    q_prod[:],
-                    q_out[:].rearrange("p h r (w i) -> p r h w i", w=2),
-                )
-                nc.sync.dma_start(out=q_dram[c, a], in_=q_out[:].rearrange("p h r d -> p h (r d)"))
+                if c == Q_CHUNKS - 1:
+                    left_to_vector.append((a, q_prod, q_out))
+                else:
+                    add_halves(
+                        nc.gpsimd,
+                        q_prod[:],
+                        q_out[:].rearrange("p h r (w i) -> p r h w i", w=2),
+                    )
+                    nc.sync.dma_start(
+                        out=q_dram[c, a], in_=q_out[:].rearrange("p h r d -> p h (r d)")
+                    )
 
-        k_acc = banks.tile([P, GROUPS, TILES, HD], F32, tag="bank")
         v_acc = banks.tile([P, GROUPS, TILES, HD], F32, tag="bank")
         for a, r in token_tiles:
-            project(k_acc[:, a, r, :], a, r, kv_words, kv_planes, 0, HD)
-        for a, r in token_tiles:
             project(v_acc[:, a, r, :], a, r, kv_words, kv_planes, HD, HD)
-        k_prod = keep.tile([P, GROUPS, TILES, 2, HD], F32, name="k_prod")
-        multiply(
-            k_acc[:].rearrange("p a r d -> p (a r) d"),
-            k_table[:].rearrange("p a r w d -> p (a r) w d"),
-            k_prod[:].rearrange("p a r w d -> p (a r) w d"),
-        )
-        k_out = keep.tile([P, GROUPS, TILES, HD], F32, name="k_out")
-        add_halves(nc.vector, k_prod[:], k_out[:].rearrange("p a r (w i) -> p a r w i", w=2))
-        nc.sync.dma_start(out=k_dram, in_=k_out[:].rearrange("p a r d -> p a (r d)"))
         v_out = keep.tile([P, GROUPS, TILES * HD], F32, name="v_out")
         nc.scalar.copy(out=v_out[:], in_=v_acc[:].rearrange("p a r d -> p a (r d)"))
         nc.sync.dma_start(out=v_dram, in_=v_out[:])
+        for a, q_prod, q_out in left_to_vector:
+            for h in range(0, CHUNK_HEADS, 2):
+                add_halves(
+                    nc.vector,
+                    q_prod[:, :, h : h + 2, :, :],
+                    q_out[:, h : h + 2, :, :].rearrange("p h r (w i) -> p r h w i", w=2),
+                )
+                nc.sync.dma_start(
+                    out=q_dram[Q_CHUNKS - 1, a][:, h : h + 2, :],
+                    in_=q_out[:, h : h + 2, :, :].rearrange("p h r d -> p h (r d)"),
+                )

@@ -12,6 +12,7 @@ FP8X4 = mybir.dt.float8_e4m3fn_x4
 FP4X4 = mybir.dt.float4_e2m1fn_x4
 MULT = mybir.AluOpType.mult
 ADD = mybir.AluOpType.add
+COPY = mybir.ActivationFunctionType.Copy
 
 P = 128
 T = 512
@@ -39,16 +40,19 @@ def tile_multiqueryattention_pa_kernel(
 ):
     nc = tc.nc
 
-    x_tiles = x.rearrange("b (a p r) k -> (b a) r p k", p=P, r=TILES)
-    sin_rows = sin.rearrange("(a p r) d -> p a (r d)", p=P, r=TILES)
-    cos_rows = cos.rearrange("(a p r) d -> p a (r d)", p=P, r=TILES)
+    x_tiles = x.rearrange("b (p a r) k -> (b a) r p k", p=P, r=TILES)
+    sin_rows = sin.rearrange("(p a r) d -> p a (r d)", p=P, r=TILES)
+    cos_rows = cos.rearrange("(p a r) d -> p a (r d)", p=P, r=TILES)
     w_words_dram = W_qkv_words.bitcast(I32).rearrange("g p n -> p g n")
     w_scales_dram = W_qkv_scales.bitcast(I32).rearrange("g (q j) n -> j q g n", j=SCALE_ROWS)
     q_dram = out_0.rearrange(
-        "b (c h) (a p r) d -> (b c) a p h (r d)", h=CHUNK_HEADS, p=P, r=TILES
+        "b (c h) (p a r) d -> (b c) a p h (r d)", h=CHUNK_HEADS, p=P, r=TILES
     )
-    k_dram = out_1.rearrange("b (a p r) d -> p (b a) (r d)", p=P, r=TILES)
-    v_dram = out_2.rearrange("b (a p r) d -> p (b a) (r d)", p=P, r=TILES)
+    q_chunk_dram = out_0.rearrange(
+        "b (c h) (p a r) d -> (b c) p h (a r d)", h=CHUNK_HEADS, p=P, r=TILES
+    )
+    k_dram = out_1.rearrange("b (p a r) d -> p (b a) (r d)", p=P, r=TILES)
+    v_dram = out_2.rearrange("b (p a r) d -> p (b a) (r d)", p=P, r=TILES)
 
     token_tiles = [(a, r) for a in range(GROUPS) for r in range(TILES)]
 
@@ -98,22 +102,14 @@ def tile_multiqueryattention_pa_kernel(
             quarters = table[:].rearrange("p a r w (s i) -> p (a r) (w s) i", s=2)
             cos_halves = cos_sb[:].rearrange("p a (r s i) -> p (a r) s i", s=2, i=HALF)
             sin_halves = sin_sb[:].rearrange("p a (r s i) -> p (a r) s i", s=2, i=HALF)
-            nc.gpsimd.tensor_scalar(
-                out=quarters[:, :, 0:4:3, :], in0=cos_halves,
-                scalar1=factor, scalar2=0.0, op0=MULT, op1=ADD,
+            nc.scalar.activation(out=quarters[:, :, 0:4:3, :], in_=cos_halves, func=COPY, scale=factor)
+            nc.scalar.activation(
+                out=quarters[:, :, 1, :], in_=sin_halves[:, :, 0, :], func=COPY, scale=-factor
             )
-            nc.gpsimd.tensor_scalar(
-                out=quarters[:, :, 1, :], in0=sin_halves[:, :, 0, :],
-                scalar1=-factor, scalar2=0.0, op0=MULT, op1=ADD,
-            )
-            nc.gpsimd.tensor_scalar(
-                out=quarters[:, :, 2, :], in0=sin_halves[:, :, 1, :],
-                scalar1=factor, scalar2=0.0, op0=MULT, op1=ADD,
+            nc.scalar.activation(
+                out=quarters[:, :, 2, :], in_=sin_halves[:, :, 1, :], func=COPY, scale=factor
             )
             return table
-
-        k_table = build_table("k_table", 1.0)
-        q_table = build_table("q_table", Q_SCALE)
 
         def warm_up(count):
             unread = banks.tile([P, CHUNK], F32, tag="bank")
@@ -193,6 +189,9 @@ def tile_multiqueryattention_pa_kernel(
             if n + 1 < len(token_tiles):
                 warm_up(1)
 
+        k_table = build_table("k_table", 1.0)
+        q_table = build_table("q_table", Q_SCALE)
+
         k_acc = banks.tile([P, GROUPS, TILES, HD], F32, tag="bank")
         for a, r in token_tiles:
             project(k_acc[:, a, r, :], a, r, kv_words, kv_planes, 0, HD)
@@ -209,6 +208,7 @@ def tile_multiqueryattention_pa_kernel(
         left_to_vector = []
         for c in range(Q_CHUNKS):
             words, planes = q_weights[c]
+            q_out = keep.tile([P, CHUNK_HEADS, GROUPS, TILES, HD], F32, name="q_out_%d" % c)
             for a in range(GROUPS):
                 q_prod = products.tile([P, TILES, CHUNK_HEADS, 2, HD], F32)
                 for r in range(TILES):
@@ -219,17 +219,25 @@ def tile_multiqueryattention_pa_kernel(
                         q_table[:, a, r, :, :].unsqueeze(1).to_broadcast([P, CHUNK_HEADS, 2, HD]),
                         q_prod[:, r, :, :, :],
                     )
-                q_out = keep.tile([P, CHUNK_HEADS, TILES, HD], F32, name="q_out_%d_%d" % (c, a))
                 if c == Q_CHUNKS - 1:
-                    left_to_vector.append((a, q_prod, q_out))
+                    left_to_vector.append((a, q_prod, q_out[:, :, a, :, :]))
                 else:
                     add_halves(
                         nc.gpsimd,
                         q_prod[:],
-                        q_out[:].rearrange("p h r (w i) -> p r h w i", w=2),
+                        q_out[:, :, a, :, :].rearrange("p h r (w i) -> p r h w i", w=2),
                     )
-                    nc.sync.dma_start(
-                        out=q_dram[c, a], in_=q_out[:].rearrange("p h r d -> p h (r d)")
+                    if c == Q_CHUNKS - 2:
+                        nc.sync.dma_start(
+                            out=q_dram[c, a],
+                            in_=q_out[:, :, a, :, :].rearrange("p h r d -> p h (r d)"),
+                        )
+            if c < Q_CHUNKS - 2:
+                for queue, h in ((nc.sync, 0), (nc.scalar, CHUNK_HEADS // 2)):
+                    heads = slice(h, h + CHUNK_HEADS // 2)
+                    queue.dma_start(
+                        out=q_chunk_dram[c][:, heads, :],
+                        in_=q_out[:, heads, :, :, :].rearrange("p h a r d -> p h (a r d)"),
                     )
 
         v_acc = banks.tile([P, GROUPS, TILES, HD], F32, tag="bank")
@@ -238,14 +246,14 @@ def tile_multiqueryattention_pa_kernel(
         v_out = keep.tile([P, GROUPS, TILES * HD], F32, name="v_out")
         nc.scalar.copy(out=v_out[:], in_=v_acc[:].rearrange("p a r d -> p a (r d)"))
         nc.sync.dma_start(out=v_dram, in_=v_out[:])
-        for a, q_prod, q_out in left_to_vector:
+        for a, q_prod, group_out in left_to_vector:
             for h in range(0, CHUNK_HEADS, 2):
                 add_halves(
                     nc.vector,
                     q_prod[:, :, h : h + 2, :, :],
-                    q_out[:, h : h + 2, :, :].rearrange("p h r (w i) -> p r h w i", w=2),
+                    group_out[:, h : h + 2, :, :].rearrange("p h r (w i) -> p r h w i", w=2),
                 )
                 nc.sync.dma_start(
                     out=q_dram[Q_CHUNKS - 1, a][:, h : h + 2, :],
-                    in_=q_out[:, h : h + 2, :, :].rearrange("p h r d -> p h (r d)"),
+                    in_=group_out[:, h : h + 2, :, :].rearrange("p h r d -> p h (r d)"),
                 )

from contextlib import ExitStack

import concourse.mybir as mybir
from concourse.masks import make_identity

F32 = mybir.dt.float32
BF16 = mybir.dt.bfloat16
I32 = mybir.dt.int32
U32 = mybir.dt.uint32
U8 = mybir.dt.uint8
FP8X4 = mybir.dt.float8_e4m3fn_x4
FP4X4 = mybir.dt.float4_e2m1fn_x4
MULT = mybir.AluOpType.mult
ADD = mybir.AluOpType.add
COPY = mybir.ActivationFunctionType.Copy

P = 128
T = 512
D = 2048
HD = 128
HALF = HD // 2
Q_HEADS = 16
PACK = 4
K_PASS = P * PACK
PASSES = D // K_PASS
CHUNK_HEADS = 4
CHUNK = CHUNK_HEADS * HD
Q_CHUNKS = Q_HEADS // CHUNK_HEADS
TILES = 2
GROUPS = T // (P * TILES)
SCALE_ROWS = 4
PSUM_BANKS = 8
Q_SCALE = HD ** -0.5

FLOPS = 2 * T * D * (Q_HEADS + 2) * HD


def tile_multiqueryattention_pa_kernel(
    tc, x, sin, cos, W_qkv_words, W_qkv_scales, out_0, out_1, out_2
):
    nc = tc.nc

    x_tiles = x.rearrange("b (p a r) k -> (b a) r p k", p=P, r=TILES)
    sin_rows = sin.rearrange("(p a r) d -> p a (r d)", p=P, r=TILES)
    cos_rows = cos.rearrange("(p a r) d -> p a (r d)", p=P, r=TILES)
    w_words_dram = W_qkv_words.bitcast(I32).rearrange("g p n -> p g n")
    w_scales_dram = W_qkv_scales.bitcast(I32).rearrange("g (q j) n -> j q g n", j=SCALE_ROWS)
    q_dram = out_0.rearrange(
        "b (c h) (p a r) d -> (b c) a p h (r d)", h=CHUNK_HEADS, p=P, r=TILES
    )
    q_chunk_dram = out_0.rearrange(
        "b (c h) (p a r) d -> (b c) p h (a r d)", h=CHUNK_HEADS, p=P, r=TILES
    )
    k_dram = out_1.rearrange("b (p a r) d -> p (b a) (r d)", p=P, r=TILES)
    v_dram = out_2.rearrange("b (p a r) d -> p (b a) (r d)", p=P, r=TILES)

    token_tiles = [(a, r) for a in range(GROUPS) for r in range(TILES)]

    with ExitStack() as ctx:
        ctx.enter_context(tc.manual_schedule())
        keep = ctx.enter_context(tc.tile_pool(name="keep", bufs=1))
        stage = ctx.enter_context(tc.tile_pool(name="stage", bufs=3))
        products = ctx.enter_context(tc.tile_pool(name="products", bufs=3))
        banks = ctx.enter_context(tc.psum_pool(name="banks", bufs=PSUM_BANKS))

        warm = keep.tile([P, CHUNK], BF16, name="warm")
        nc.vector.memset(warm[:], 0.0)

        def load_weight_columns(name, first, width):
            planes = keep.tile([P, PASSES, width], U8, name="planes_" + name, align_bytes=64)
            nc.vector.memset(planes[:].bitcast(I32), 0)
            for j in range(SCALE_ROWS):
                nc.sync.dma_start(
                    out=planes[:].bitcast(I32)[j:P:32, :, :],
                    in_=w_scales_dram[j, :, :, first // 4 : (first + width) // 4],
                )
            words = keep.tile([P, PASSES, 2 * width], U8, name="words_" + name, align_bytes=64)
            nc.sync.dma_start(
                out=words[:].bitcast(I32),
                in_=w_words_dram[:, :, first // 2 : (first + width) // 2],
            )
            return words, planes

        x_sb = {}
        for a, r in token_tiles:
            x_sb[a, r] = keep.tile([P, D], BF16, name="x_%d_%d" % (a, r))
            nc.sync.dma_start(out=x_sb[a, r][:], in_=x_tiles[a, r])
        kv_words, kv_planes = load_weight_columns("kv", Q_HEADS * HD, 2 * HD)
        sin_sb = keep.tile([P, GROUPS, TILES * HD], BF16, name="sin_sb")
        cos_sb = keep.tile([P, GROUPS, TILES * HD], BF16, name="cos_sb")
        nc.sync.dma_start(out=sin_sb[:], in_=sin_rows)
        nc.sync.dma_start(out=cos_sb[:], in_=cos_rows)
        q_weights = [
            load_weight_columns("q%d" % c, c * CHUNK, CHUNK) for c in range(Q_CHUNKS)
        ]

        identity = keep.tile([P, P], F32, name="identity")
        make_identity(nc, identity[:])

        def build_table(name, factor):
            table = keep.tile([P, GROUPS, TILES, 2, HD], F32, name=name)
            quarters = table[:].rearrange("p a r w (s i) -> p (a r) (w s) i", s=2)
            cos_halves = cos_sb[:].rearrange("p a (r s i) -> p (a r) s i", s=2, i=HALF)
            sin_halves = sin_sb[:].rearrange("p a (r s i) -> p (a r) s i", s=2, i=HALF)
            nc.scalar.activation(out=quarters[:, :, 0:4:3, :], in_=cos_halves, func=COPY, scale=factor)
            nc.scalar.activation(
                out=quarters[:, :, 1, :], in_=sin_halves[:, :, 0, :], func=COPY, scale=-factor
            )
            nc.scalar.activation(
                out=quarters[:, :, 2, :], in_=sin_halves[:, :, 1, :], func=COPY, scale=factor
            )
            return table

        def warm_up(count):
            unread = banks.tile([P, CHUNK], F32, tag="bank")
            for n in range(count):
                nc.tensor.matmul(
                    out=unread[:], lhsT=warm[:, 0:P], rhs=warm[:], start=True, stop=True
                )

        x_sorted = {}
        x_codes = {}
        x_scales = {}

        def sort_words(a, r):
            x_sorted[a, r] = keep.tile([P, PASSES, 2, P], F32, name="x_sorted_%d_%d" % (a, r))
            nc.vector.tensor_copy(
                out=x_sorted[a, r][:],
                in_=x_sb[a, r][:].bitcast(F32).rearrange("t (g p u) -> t g u p", p=P, u=2),
            )

        def quantise_tokens(a, r):
            codes = keep.tile([P, PASSES, P], U32, name="x_codes_%d_%d" % (a, r), align_bytes=64)
            scales = keep.tile([P, PASSES, P], U8, name="x_scales_%d_%d" % (a, r), align_bytes=64)
            for first_pass in range(0, PASSES, 2):
                two_passes = slice(first_pass, first_pass + 2)
                turned = banks.tile([P, 2, 2, P], F32, tag="bank")
                for g in range(2):
                    for u in range(2):
                        nc.tensor.transpose(
                            turned[:, g, u, :], x_sorted[a, r][:, first_pass + g, u, :], identity[:]
                        )
                grouped = stage.tile([P, 2, P, PACK], BF16, align_bytes=64)
                nc.scalar.copy(
                    out=grouped[:].bitcast(F32), in_=turned[:].rearrange("p g u t -> p g t u")
                )
                nc.vector.quantize_mx(
                    out=codes[:, two_passes, :].rearrange("p g t -> p (g t)").bitcast(FP8X4),
                    scales=scales[:, two_passes, :].rearrange("p g t -> p (g t)"),
                    in_=grouped[:].rearrange("p g t e -> p (g t e)"),
                )
            x_codes[a, r] = codes
            x_scales[a, r] = scales

        def project(acc, a, r, words, planes, first, width):
            for g in range(PASSES):
                nc.tensor.matmul_mx(
                    out=acc,
                    lhsT=x_codes[a, r][:, g, :].bitcast(FP8X4),
                    lhsT_scale=x_scales[a, r][:, g, :],
                    rhs=words[:, g, 2 * first : 2 * (first + width)].bitcast(FP4X4),
                    rhs_scale=planes[:, g, first : first + width],
                    start=(g == 0),
                    stop=(g == PASSES - 1),
                )

        def multiply(vectors, table, prod):
            nc.vector.tensor_tensor(
                out=prod,
                in0=vectors.unsqueeze(2).to_broadcast(list(prod.shape)),
                in1=table,
                op=MULT,
            )

        def add_halves(engine, prod, rotated):
            engine.tensor_tensor(
                out=rotated,
                in0=prod[:, :, :, :, 0:HALF],
                in1=prod[:, :, :, :, HALF:HD],
                op=ADD,
            )

        warm_up(6)
        sort_words(*token_tiles[0])
        for n, (a, r) in enumerate(token_tiles):
            if n + 1 < len(token_tiles):
                sort_words(*token_tiles[n + 1])
            quantise_tokens(a, r)
            if n + 1 < len(token_tiles):
                warm_up(1)

        k_table = build_table("k_table", 1.0)
        q_table = build_table("q_table", Q_SCALE)

        k_acc = banks.tile([P, GROUPS, TILES, HD], F32, tag="bank")
        for a, r in token_tiles:
            project(k_acc[:, a, r, :], a, r, kv_words, kv_planes, 0, HD)
        k_prod = keep.tile([P, GROUPS, TILES, 2, HD], F32, name="k_prod")
        multiply(
            k_acc[:].rearrange("p a r d -> p (a r) d"),
            k_table[:].rearrange("p a r w d -> p (a r) w d"),
            k_prod[:].rearrange("p a r w d -> p (a r) w d"),
        )
        k_out = keep.tile([P, GROUPS, TILES, HD], F32, name="k_out")
        add_halves(nc.gpsimd, k_prod[:], k_out[:].rearrange("p a r (w i) -> p a r w i", w=2))
        nc.sync.dma_start(out=k_dram, in_=k_out[:].rearrange("p a r d -> p a (r d)"))

        left_to_vector = []
        for c in range(Q_CHUNKS):
            words, planes = q_weights[c]
            q_out = keep.tile([P, CHUNK_HEADS, GROUPS, TILES, HD], F32, name="q_out_%d" % c)
            for a in range(GROUPS):
                q_prod = products.tile([P, TILES, CHUNK_HEADS, 2, HD], F32)
                for r in range(TILES):
                    acc = banks.tile([P, CHUNK], F32, tag="bank")
                    project(acc[:], a, r, words, planes, 0, CHUNK)
                    multiply(
                        acc[:].rearrange("p (h d) -> p h d", d=HD),
                        q_table[:, a, r, :, :].unsqueeze(1).to_broadcast([P, CHUNK_HEADS, 2, HD]),
                        q_prod[:, r, :, :, :],
                    )
                if c == Q_CHUNKS - 1:
                    left_to_vector.append((a, q_prod, q_out[:, :, a, :, :]))
                else:
                    add_halves(
                        nc.gpsimd,
                        q_prod[:],
                        q_out[:, :, a, :, :].rearrange("p h r (w i) -> p r h w i", w=2),
                    )
                    if c == Q_CHUNKS - 2:
                        nc.sync.dma_start(
                            out=q_dram[c, a],
                            in_=q_out[:, :, a, :, :].rearrange("p h r d -> p h (r d)"),
                        )
            if c < Q_CHUNKS - 2:
                for queue, h in ((nc.sync, 0), (nc.scalar, CHUNK_HEADS // 2)):
                    heads = slice(h, h + CHUNK_HEADS // 2)
                    queue.dma_start(
                        out=q_chunk_dram[c][:, heads, :],
                        in_=q_out[:, heads, :, :, :].rearrange("p h a r d -> p h (a r d)"),
                    )

        v_acc = banks.tile([P, GROUPS, TILES, HD], F32, tag="bank")
        for a, r in token_tiles:
            project(v_acc[:, a, r, :], a, r, kv_words, kv_planes, HD, HD)
        v_out = keep.tile([P, GROUPS, TILES * HD], F32, name="v_out")
        nc.scalar.copy(out=v_out[:], in_=v_acc[:].rearrange("p a r d -> p a (r d)"))
        nc.sync.dma_start(out=v_dram, in_=v_out[:])
        for a, q_prod, group_out in left_to_vector:
            for h in range(0, CHUNK_HEADS, 2):
                add_halves(
                    nc.vector,
                    q_prod[:, :, h : h + 2, :, :],
                    group_out[:, h : h + 2, :, :].rearrange("p h r (w i) -> p r h w i", w=2),
                )
                nc.sync.dma_start(
                    out=q_dram[Q_CHUNKS - 1, a][:, h : h + 2, :],
                    in_=group_out[:, h : h + 2, :, :].rearrange("p h r d -> p h (r d)"),
                )
